import numpy as np
import ml_dtypes


def mxq(x, axis, fmt="e4m3"):
    dtype, down = {"e4m3": (ml_dtypes.float8_e4m3fn, 7), "e5m2": (ml_dtypes.float8_e5m2, 14)}[fmt]
    v = np.moveaxis(np.asarray(x, np.float32).astype(ml_dtypes.bfloat16).astype(np.float64), axis, -1)
    blocks = v.reshape(v.shape[:-1] + (-1, 32))
    amax = np.abs(blocks).max(-1, keepdims=True)
    byte = np.maximum(np.where(amax > 0, np.frexp(amax)[1] - 1 + 127, 0) - down, 1)
    scale = np.exp2(byte - 127.0)
    codes = (blocks / scale).astype(np.float32).astype(dtype).astype(np.float64)
    return np.moveaxis((codes * scale).reshape(v.shape), -1, axis)


WIDE = False


def mx_kscale(k):
    if not WIDE:
        return np.ones(k)
    levels = np.array([10, -10, 5, -5, 0])
    if k % 512:
        return np.exp2(np.random.permutation(np.resize(levels, k // 32))).repeat(32)
    a = np.empty((k // 512, 16))
    for p in range(k // 512):
        a[p, :8] = np.random.permutation(np.resize(levels, 8))
        for g in range(8):
            far = levels[np.abs(levels - a[p, g]) >= 10]
            a[p, g + 8] = far[np.random.randint(len(far))]
    return np.exp2(a.ravel()).repeat(32)


BF16 = ml_dtypes.bfloat16


def bf(x):
    return np.asarray(x, np.float32).astype(BF16)


def f64(x):
    return np.asarray(x).astype(np.float64)


N, M, P = 128, 8, 16384
EPS = 1e-6


def setup_inputs():
    s = mx_kscale(P)
    a = np.log2(s) / 10.0
    u, v = np.maximum(a, 0.0), np.maximum(-a, 0.0)
    x = np.random.standard_normal((N * M, P)).reshape(N, M, P)
    x[0::2] = (x[0::2] + u) * s
    x[1::2] = (x[1::2] + v) / s
    nrm = np.sqrt(N / 2.0 * np.sum(s ** 2.0 * (1.0 / M + u * u) + s ** -2.0 * (1.0 / M + v * v)))
    q = 0.5 * (np.sum(u * u) + np.sum(v * v))
    sd = np.sqrt((P + q) / M + q) / nrm
    return {"inputs": bf(x.reshape(N * M, P)),
            "w": bf(-(0.2 + 0.1 * np.random.random(1)) / sd),
            "b": bf(0.5 + 0.1 * np.random.standard_normal(1))}


def reference(inputs, w, b):
    e = f64(inputs).reshape(N, M, P)
    cmean = np.mean(e, axis=1)
    norm = np.sqrt(np.maximum(np.sum(cmean * cmean), EPS))
    centroids = cmean / norm
    S = (mxq(e, 2, "e4m3") @ mxq(centroids, 1, "e4m3").T).reshape(N * M, N)
    return np.clip(np.abs(f64(w)) * S + f64(b), 0.0, 1.0)

@@ -1,0 +1,256 @@
+import concourse.mybir as mybir
+from concourse.masks import make_identity
+
+F32 = mybir.dt.float32
+BF16 = mybir.dt.bfloat16
+U32 = mybir.dt.uint32
+U8 = mybir.dt.uint8
+I32 = mybir.dt.int32
+FP8X4 = mybir.dt.float8_e4m3fn_x4
+ALU = mybir.AluOpType
+ACT = mybir.ActivationFunctionType
+AXIS_X = mybir.AxisListType.X
+
+P = 128
+PACK = 4
+K_PASS = P * PACK
+
+ROWS = 1024
+FEATURES = 16384
+SPEAKERS = 128
+UTTERANCES = 8
+EPS = 1e-6
+
+ROW_TILES = ROWS // P
+TILE_SPEAKERS = P // UTTERANCES
+CHUNK_PASSES = 4
+CHUNK_K = CHUNK_PASSES * K_PASS
+CHUNKS = FEATURES // CHUNK_K
+UNITS = CHUNKS * ROW_TILES
+BANK_PASSES = 2
+PLANES_PER_TILE = 4
+VECTOR_SUM_PASSES = 1
+START_PASSES = 6
+
+FLOPS = 2 * ROWS * SPEAKERS * FEATURES
+
+
+def idle_pass(nc, pool, codes, scales):
+    idle_out = pool.tile([P, CHUNK_PASSES * P], F32)
+    nc.tensor.matmul_mx(
+        out=idle_out[:],
+        lhsT=codes[:, 0:P].bitcast(FP8X4),
+        lhsT_scale=scales[:, 0:P],
+        rhs=codes[:].bitcast(FP8X4),
+        rhs_scale=scales[:],
+        start=True,
+        stop=True,
+    )
+
+
+def tile_similaritymatrixlayer_k_kernel(tc, inputs, w, b, out):
+    nc = tc.nc
+    with tc.manual_schedule(), tc.tile_pool(name="keep", bufs=1) as keep:
+        x_codes = keep.tile([P, CHUNKS, ROW_TILES, CHUNK_PASSES, P], U32, align_bytes=64)
+        x_scales = keep.tile([P, UNITS // PLANES_PER_TILE, CHUNK_PASSES * P], U8, align_bytes=64)
+        spk_sum = keep.tile([P, CHUNKS, ROW_TILES, CHUNK_PASSES, TILE_SPEAKERS * PACK], F32)
+        sq_part = keep.tile([P, UNITS], F32)
+
+        ident = keep.tile([P, P], F32)
+        make_identity(nc, ident[:])
+        ones = keep.tile([P, P], F32)
+        nc.vector.memset(ones[:], 1.0)
+        warm = keep.tile([P, 1], F32)
+        nc.scalar.sqrt(out=warm[:], in_=ones[:, 0:1])
+        w_bf = keep.tile([P, 1], BF16)
+        b_bf = keep.tile([P, 1], BF16)
+        nc.scalar.dma_start(out=w_bf[:], in_=w.partition_broadcast(P))
+        nc.scalar.dma_start(out=b_bf[:], in_=b.partition_broadcast(P))
+        inv_norm = keep.tile([P, 1], F32)
+        idle_codes = keep.tile([P, CHUNK_PASSES * P], U32, align_bytes=64)
+        idle_scales = keep.tile([P, CHUNK_PASSES * P], U8, align_bytes=64)
+
+        def plane_of(c, r):
+            unit = c * ROW_TILES + r
+            return x_scales[PACK * (unit % PLANES_PER_TILE) : P, unit // PLANES_PER_TILE, :]
+
+        with (
+            tc.tile_pool(name="xin", bufs=4) as xin,
+            tc.tile_pool(name="stage", bufs=3) as stage,
+            tc.tile_pool(name="scrap", bufs=2) as scrap,
+            tc.psum_pool(name="ps_x", bufs=4) as ps_x,
+            tc.psum_pool(name="ps_s", bufs=2) as ps_s,
+            tc.psum_pool(name="ps_n", bufs=1) as ps_n,
+            tc.psum_pool(name="ps_w", bufs=1) as ps_w,
+        ):
+            idle_src = stage.tile([P, CHUNK_PASSES, P, PACK], BF16, align_bytes=64, tag="grouped")
+            nc.vector.memset(idle_src[:].bitcast(I32), 0)
+            nc.vector.quantize_mx(
+                out=idle_codes[:].bitcast(FP8X4),
+                scales=idle_scales[:],
+                in_=idle_src[:].rearrange("p g i t -> p (g i t)"),
+            )
+            for i in range(START_PASSES):
+                idle_pass(nc, ps_w, idle_codes, idle_scales)
+
+            member_f32 = keep.tile([P, TILE_SPEAKERS], F32)
+            nc.vector.tensor_reduce(
+                out=member_f32[:],
+                in_=ident[:].rearrange("p (s m) -> p s m", m=UTTERANCES),
+                axis=AXIS_X,
+                op=ALU.add,
+            )
+            member = keep.tile([P, TILE_SPEAKERS], BF16)
+            nc.vector.tensor_copy(out=member[:], in_=member_f32[:])
+
+            def square_unit(unit):
+                squares = scrap.tile([P, CHUNK_PASSES * TILE_SPEAKERS * PACK], BF16)
+                nc.scalar.activation(
+                    out=squares[:],
+                    in_=spk_sum[:, unit // ROW_TILES, unit % ROW_TILES, :, :].rearrange(
+                        "p g x -> p (g x)"
+                    ),
+                    func=ACT.Square,
+                    accum_out=sq_part[:, unit : unit + 1],
+                )
+
+            for unit in range(UNITS):
+                c = unit // ROW_TILES
+                r = unit % ROW_TILES
+                x_sb = xin.tile([P, CHUNK_K], BF16)
+                nc.sync.dma_start(
+                    out=x_sb[:], in_=inputs[r * P : (r + 1) * P, c * CHUNK_K : (c + 1) * CHUNK_K]
+                )
+                x_words = x_sb[:].bitcast(F32)
+                x_quads = x_sb[:].rearrange("p (q t) -> p q t", t=PACK)
+                grouped = stage.tile([P, CHUNK_PASSES, P, PACK], BF16, align_bytes=64)
+                grouped_words = grouped[:].bitcast(F32)
+                for h in range(CHUNK_PASSES // BANK_PASSES):
+                    xt = ps_x.tile([P, BANK_PASSES, 2, P], F32)
+                    for g in range(BANK_PASSES):
+                        for u in range(2):
+                            first = (h * BANK_PASSES + g) * 2 * P
+                            nc.tensor.transpose(
+                                xt[:, g, u, :], x_words[:, first + u : first + 2 * P : 2], ident[:]
+                            )
+                    nc.scalar.copy(
+                        out=grouped_words[:, h * BANK_PASSES : (h + 1) * BANK_PASSES, :, :],
+                        in_=xt[:].rearrange("p g u i -> p g i u"),
+                    )
+                if unit > 0:
+                    square_unit(unit - 1)
+
+                sums = ps_s.tile([P, CHUNK_PASSES - VECTOR_SUM_PASSES, PACK, TILE_SPEAKERS], F32)
+                for g in range(VECTOR_SUM_PASSES, CHUNK_PASSES):
+                    for t in range(PACK):
+                        nc.tensor.matmul(
+                            sums[:, g - VECTOR_SUM_PASSES, t, :],
+                            lhsT=x_quads[:, g * P : (g + 1) * P, t],
+                            rhs=member[:],
+                            start=True,
+                            stop=True,
+                        )
+                    if g == VECTOR_SUM_PASSES:
+                        idle_pass(nc, ps_w, idle_codes, idle_scales)
+
+                nc.vector.tensor_reduce(
+                    out=spk_sum[:, c, r, 0:VECTOR_SUM_PASSES, :].rearrange(
+                        "p g (s t) -> p (g s) t", t=PACK
+                    ),
+                    in_=grouped[:, 0:VECTOR_SUM_PASSES, :, :].rearrange(
+                        "p g (s m) t -> p (g s) t m", m=UTTERANCES
+                    ),
+                    axis=AXIS_X,
+                    op=ALU.add,
+                )
+                nc.vector.tensor_copy(
+                    out=spk_sum[:, c, r, VECTOR_SUM_PASSES:CHUNK_PASSES, :].rearrange(
+                        "p g (s t) -> p g s t", t=PACK
+                    ),
+                    in_=sums[:].rearrange("p g t s -> p g s t"),
+                )
+                nc.vector.quantize_mx(
+                    out=x_codes[:, c, r, :, :].rearrange("p g i -> p (g i)").bitcast(FP8X4),
+                    scales=plane_of(c, r),
+                    in_=grouped[:].rearrange("p g i t -> p (g i t)"),
+                )
+            square_unit(UNITS - 1)
+
+            sq_lane = keep.tile([P, 1], F32)
+            nc.vector.tensor_reduce(out=sq_lane[:], in_=sq_part[:], axis=AXIS_X, op=ALU.add)
+            total = ps_n.tile([P, 1], F32)
+            nc.tensor.matmul(total[:], lhsT=ones[:], rhs=sq_lane[:], start=True, stop=True)
+            floored = keep.tile([P, 1], F32)
+            nc.vector.tensor_scalar_max(
+                out=floored[:], in0=total[:], scalar1=UTTERANCES * UTTERANCES * EPS
+            )
+            norm8 = keep.tile([P, 1], F32)
+            nc.scalar.sqrt(out=norm8[:], in_=floored[:])
+            nc.vector.reciprocal(out=inv_norm[:], in_=norm8[:])
+
+        with (
+            tc.tile_pool(name="cen", bufs=1) as cen,
+            tc.tile_pool(name="cstage", bufs=3) as cstage,
+            tc.psum_pool(name="ps_acc", bufs=1) as ps_acc,
+        ):
+            c_codes = cen.tile([P, CHUNKS, CHUNK_PASSES, SPEAKERS], U32, align_bytes=64)
+            c_scales = cen.tile([P, CHUNKS, CHUNK_PASSES, SPEAKERS], U8, align_bytes=64)
+            result = cen.tile([P, ROW_TILES, SPEAKERS], F32)
+            acc = [ps_acc.tile([P, SPEAKERS], F32, name="acc%d" % r) for r in range(ROW_TILES)]
+
+            def quantise_centroids(c, g):
+                c_bf = cstage.tile([P, ROW_TILES, TILE_SPEAKERS * PACK], BF16, align_bytes=64)
+                if g % 2 == 0:
+                    nc.vector.tensor_scalar_mul(
+                        out=c_bf[:], in0=spk_sum[:, c, :, g, :], scalar1=inv_norm[:, 0:1]
+                    )
+                else:
+                    nc.scalar.activation(
+                        out=c_bf[:], in_=spk_sum[:, c, :, g, :], func=ACT.Copy, scale=inv_norm[:, 0:1]
+                    )
+                nc.vector.quantize_mx(
+                    out=c_codes[:, c, g, :].bitcast(FP8X4),
+                    scales=c_scales[:, c, g, :],
+                    in_=c_bf[:].rearrange("p r x -> p (r x)"),
+                )
+
+            def product_pass(c, g, r):
+                nc.tensor.matmul_mx(
+                    out=acc[r][:],
+                    lhsT=x_codes[:, c, r, g, :].bitcast(FP8X4),
+                    lhsT_scale=plane_of(c, r)[:, g * P : (g + 1) * P],
+                    rhs=c_codes[:, c, g, :].bitcast(FP8X4),
+                    rhs_scale=c_scales[:, c, g, :],
+                    start=(c == 0 and g == 0),
+                    stop=(c == CHUNKS - 1 and g == CHUNK_PASSES - 1),
+                )
+
+            for c in range(CHUNKS - 1):
+                for g in range(CHUNK_PASSES):
+                    quantise_centroids(c, g)
+                    for r in range(ROW_TILES):
+                        product_pass(c, g, r)
+
+            w_pos = keep.tile([P, 1], F32)
+            w_neg = keep.tile([P, 1], F32)
+            w_abs = keep.tile([P, 1], F32)
+            b_f32 = keep.tile([P, 1], F32)
+            nc.vector.tensor_copy(out=w_pos[:], in_=w_bf[:])
+            nc.vector.tensor_scalar_mul(out=w_neg[:], in0=w_pos[:], scalar1=-1.0)
+            nc.vector.tensor_tensor(out=w_abs[:], in0=w_pos[:], in1=w_neg[:], op=ALU.max)
+            nc.vector.tensor_copy(out=b_f32[:], in_=b_bf[:])
+
+            for g in range(CHUNK_PASSES):
+                quantise_centroids(CHUNKS - 1, g)
+            for r in range(ROW_TILES):
+                for g in range(CHUNK_PASSES):
+                    product_pass(CHUNKS - 1, g, r)
+                nc.scalar.activation(
+                    out=result[:, r, :],
+                    in_=acc[r][:],
+                    func=ACT.Relu,
+                    bias=b_f32[:, 0:1],
+                    scale=w_abs[:, 0:1],
+                )
+                nc.vector.tensor_scalar_min(out=result[:, r, :], in0=result[:, r, :], scalar1=1.0)
+                nc.sync.dma_start(out=out[r * P : (r + 1) * P, :], in_=result[:, r, :])

@@ -150,8 +150,6 @@ def tile_similaritymatrixlayer_k_kernel(tc, inputs, w, b, out):
                             start=True,
                             stop=True,
                         )
-                    if g == VECTOR_SUM_PASSES:
-                        idle_pass(nc, ps_w, idle_codes, idle_scales)
 
                 nc.vector.tensor_reduce(
                     out=spk_sum[:, c, r, 0:VECTOR_SUM_PASSES, :].rearrange(

@@ -13,6 +13,7 @@ AXIS_X = mybir.AxisListType.X
 
 P = 128
 PACK = 4
+BLOCK = 32
 K_PASS = P * PACK
 
 ROWS = 1024
@@ -29,10 +30,15 @@ CHUNKS = FEATURES // CHUNK_K
 UNITS = CHUNKS * ROW_TILES
 BANK_PASSES = 2
 PLANES_PER_TILE = 4
-VECTOR_SUM_PASSES = 1
+PERM_PASSES = 1
+LOADS_AHEAD = 3
 START_PASSES = 6
 
 FLOPS = 2 * ROWS * SPEAKERS * FEATURES
+
+
+def vector_passes(unit):
+    return 0 if unit % 5 == 3 and unit > 5 else 1
 
 
 def idle_pass(nc, pool, codes, scales):
@@ -76,6 +82,7 @@ def tile_similaritymatrixlayer_k_kernel(tc, inputs, w, b, out):
 
         with (
             tc.tile_pool(name="xin", bufs=4) as xin,
+            tc.tile_pool(name="perms", bufs=3) as perms,
             tc.tile_pool(name="stage", bufs=3) as stage,
             tc.tile_pool(name="scrap", bufs=2) as scrap,
             tc.psum_pool(name="ps_x", bufs=4) as ps_x,
@@ -114,64 +121,112 @@ def tile_similaritymatrixlayer_k_kernel(tc, inputs, w, b, out):
                     accum_out=sq_part[:, unit : unit + 1],
                 )
 
-            for unit in range(UNITS):
-                c = unit // ROW_TILES
-                r = unit % ROW_TILES
+            x_tiles = {}
+            perm_tiles = {}
+            grouped_tiles = {}
+            sum_tiles = {}
+
+            def load(unit):
+                c, r = divmod(unit, ROW_TILES)
                 x_sb = xin.tile([P, CHUNK_K], BF16)
                 nc.sync.dma_start(
                     out=x_sb[:], in_=inputs[r * P : (r + 1) * P, c * CHUNK_K : (c + 1) * CHUNK_K]
                 )
+                x_tiles[unit] = x_sb
+
+            def permute(unit):
+                x_sb = x_tiles[unit]
+                perm = perms.tile([P, 2, PERM_PASSES * K_PASS // 2], BF16)
+                nc.vector.tensor_copy(
+                    out=perm[:].rearrange("p u (b e) -> p u b e", e=BLOCK // 2),
+                    in_=x_sb[:, (CHUNK_PASSES - PERM_PASSES) * K_PASS :].rearrange(
+                        "p (b u e) -> p u b e", u=2, e=BLOCK // 2
+                    ),
+                )
+                perm_tiles[unit] = perm
+
+            def transposes(unit):
+                x_sb = x_tiles[unit]
                 x_words = x_sb[:].bitcast(F32)
-                x_quads = x_sb[:].rearrange("p (q t) -> p q t", t=PACK)
-                grouped = stage.tile([P, CHUNK_PASSES, P, PACK], BF16, align_bytes=64)
+                grouped = stage.tile([P, CHUNK_PASSES, P, PACK], BF16, align_bytes=64, tag="grouped")
                 grouped_words = grouped[:].bitcast(F32)
                 for h in range(CHUNK_PASSES // BANK_PASSES):
                     xt = ps_x.tile([P, BANK_PASSES, 2, P], F32)
-                    for g in range(BANK_PASSES):
+                    for i in range(BANK_PASSES):
+                        g = h * BANK_PASSES + i
                         for u in range(2):
-                            first = (h * BANK_PASSES + g) * 2 * P
-                            nc.tensor.transpose(
-                                xt[:, g, u, :], x_words[:, first + u : first + 2 * P : 2], ident[:]
-                            )
+                            if g < CHUNK_PASSES - PERM_PASSES:
+                                first = g * 2 * P + u
+                                words = x_words[:, first : (g + 1) * 2 * P : 2]
+                            else:
+                                j = g - (CHUNK_PASSES - PERM_PASSES)
+                                words = perm_tiles[unit][:].bitcast(F32)[:, u, j * P : (j + 1) * P]
+                            nc.tensor.transpose(xt[:, i, u, :], words, ident[:])
                     nc.scalar.copy(
                         out=grouped_words[:, h * BANK_PASSES : (h + 1) * BANK_PASSES, :, :],
                         in_=xt[:].rearrange("p g u i -> p g i u"),
                     )
-                if unit > 0:
-                    square_unit(unit - 1)
+                grouped_tiles[unit] = grouped
 
-                sums = ps_s.tile([P, CHUNK_PASSES - VECTOR_SUM_PASSES, PACK, TILE_SPEAKERS], F32)
-                for g in range(VECTOR_SUM_PASSES, CHUNK_PASSES):
+            def tensor_sums(unit):
+                x_quads = x_tiles[unit][:].rearrange("p (q t) -> p q t", t=PACK)
+                sums = ps_s.tile([P, CHUNK_PASSES, PACK, TILE_SPEAKERS], F32)
+                for g in range(vector_passes(unit), CHUNK_PASSES):
                     for t in range(PACK):
+                        if g < CHUNK_PASSES - PERM_PASSES:
+                            lhsT = x_quads[:, g * P : (g + 1) * P, t]
+                        else:
+                            j = g - (CHUNK_PASSES - PERM_PASSES)
+                            perm_pairs = perm_tiles[unit][:].rearrange("p u (q e) -> p u q e", e=2)
+                            lhsT = perm_pairs[:, t // 2, j * P : (j + 1) * P, t % 2]
                         nc.tensor.matmul(
-                            sums[:, g - VECTOR_SUM_PASSES, t, :],
-                            lhsT=x_quads[:, g * P : (g + 1) * P, t],
-                            rhs=member[:],
-                            start=True,
-                            stop=True,
+                            sums[:, g, t, :], lhsT=lhsT, rhs=member[:], start=True, stop=True
                         )
+                sum_tiles[unit] = sums
 
-                nc.vector.tensor_reduce(
-                    out=spk_sum[:, c, r, 0:VECTOR_SUM_PASSES, :].rearrange(
-                        "p g (s t) -> p (g s) t", t=PACK
-                    ),
-                    in_=grouped[:, 0:VECTOR_SUM_PASSES, :, :].rearrange(
-                        "p g (s m) t -> p (g s) t m", m=UTTERANCES
-                    ),
-                    axis=AXIS_X,
-                    op=ALU.add,
-                )
-                nc.vector.tensor_copy(
-                    out=spk_sum[:, c, r, VECTOR_SUM_PASSES:CHUNK_PASSES, :].rearrange(
-                        "p g (s t) -> p g s t", t=PACK
-                    ),
-                    in_=sums[:].rearrange("p g t s -> p g s t"),
-                )
+            def vector_work(unit):
+                c, r = divmod(unit, ROW_TILES)
+                first = vector_passes(unit)
+                grouped = grouped_tiles.pop(unit)
                 nc.vector.quantize_mx(
                     out=x_codes[:, c, r, :, :].rearrange("p g i -> p (g i)").bitcast(FP8X4),
                     scales=plane_of(c, r),
                     in_=grouped[:].rearrange("p g i t -> p (g i t)"),
                 )
+                nc.vector.tensor_copy(
+                    out=spk_sum[:, c, r, first:CHUNK_PASSES, :].rearrange(
+                        "p g (s t) -> p g s t", t=PACK
+                    ),
+                    in_=sum_tiles.pop(unit)[:, first:CHUNK_PASSES, :, :].rearrange(
+                        "p g t s -> p g s t"
+                    ),
+                )
+                if first:
+                    nc.vector.tensor_reduce(
+                        out=spk_sum[:, c, r, 0:first, :].rearrange("p g (s t) -> p (g s) t", t=PACK),
+                        in_=grouped[:, 0:first, :, :].rearrange(
+                            "p g (s m) t -> p (g s) t m", m=UTTERANCES
+                        ),
+                        axis=AXIS_X,
+                        op=ALU.add,
+                    )
+
+            for unit in range(LOADS_AHEAD):
+                load(unit)
+            permute(0)
+            for unit in range(UNITS + 1):
+                if unit + LOADS_AHEAD < UNITS:
+                    load(unit + LOADS_AHEAD)
+                if unit + 1 < UNITS:
+                    permute(unit + 1)
+                if unit < UNITS:
+                    transposes(unit)
+                if unit >= 2:
+                    square_unit(unit - 2)
+                if unit < UNITS:
+                    tensor_sums(unit)
+                if unit >= 1:
+                    vector_work(unit - 1)
             square_unit(UNITS - 1)
 
             sq_lane = keep.tile([P, 1], F32)

@@ -30,7 +30,8 @@ CHUNKS = FEATURES // CHUNK_K
 UNITS = CHUNKS * ROW_TILES
 BANK_PASSES = 2
 PLANES_PER_TILE = 4
-PERM_PASSES = 1
+PERM_FIRST = 1
+PERM_VECTOR = 2
 LOADS_AHEAD = 3
 START_PASSES = 6
 
@@ -82,7 +83,7 @@ def tile_similaritymatrixlayer_k_kernel(tc, inputs, w, b, out):
 
         with (
             tc.tile_pool(name="xin", bufs=4) as xin,
-            tc.tile_pool(name="perms", bufs=3) as perms,
+            tc.tile_pool(name="perms", bufs=2) as perms,
             tc.tile_pool(name="stage", bufs=3) as stage,
             tc.tile_pool(name="scrap", bufs=2) as scrap,
             tc.psum_pool(name="ps_x", bufs=4) as ps_x,
@@ -135,15 +136,25 @@ def tile_similaritymatrixlayer_k_kernel(tc, inputs, w, b, out):
                 x_tiles[unit] = x_sb
 
             def permute(unit):
-                x_sb = x_tiles[unit]
-                perm = perms.tile([P, 2, PERM_PASSES * K_PASS // 2], BF16)
-                nc.vector.tensor_copy(
-                    out=perm[:].rearrange("p u (b e) -> p u b e", e=BLOCK // 2),
-                    in_=x_sb[:, (CHUNK_PASSES - PERM_PASSES) * K_PASS :].rearrange(
+                for first, last, pool, tag in (
+                    (PERM_FIRST, PERM_VECTOR, perms, "perm_g"),
+                    (PERM_VECTOR, CHUNK_PASSES, perms, "perm_v"),
+                ):
+                    width = (last - first) * K_PASS // 2
+                    perm = pool.tile([P, 2, width], BF16, tag=tag)
+                    dst = perm[:].rearrange("p u (b e) -> p u b e", e=BLOCK // 2)
+                    src = x_tiles[unit][:, first * K_PASS : last * K_PASS].rearrange(
                         "p (b u e) -> p u b e", u=2, e=BLOCK // 2
-                    ),
-                )
-                perm_tiles[unit] = perm
+                    )
+                    if tag == "perm_g":
+                        nc.gpsimd.tensor_scalar(
+                            out=dst, in0=src, scalar1=1.0, scalar2=0.0, op0=ALU.mult, op1=ALU.add
+                        )
+                    else:
+                        nc.vector.tensor_copy(out=dst, in_=src)
+                    for g in range(first, last):
+                        j = (g - first) * K_PASS // 2
+                        perm_tiles[unit, g] = perm[:, :, j : j + K_PASS // 2]
 
             def transposes(unit):
                 x_sb = x_tiles[unit]
@@ -155,12 +166,11 @@ def tile_similaritymatrixlayer_k_kernel(tc, inputs, w, b, out):
                     for i in range(BANK_PASSES):
                         g = h * BANK_PASSES + i
                         for u in range(2):
-                            if g < CHUNK_PASSES - PERM_PASSES:
+                            if g < PERM_FIRST:
                                 first = g * 2 * P + u
                                 words = x_words[:, first : (g + 1) * 2 * P : 2]
                             else:
-                                j = g - (CHUNK_PASSES - PERM_PASSES)
-                                words = perm_tiles[unit][:].bitcast(F32)[:, u, j * P : (j + 1) * P]
+                                words = perm_tiles[unit, g][:, u, :].bitcast(F32)
                             nc.tensor.transpose(xt[:, i, u, :], words, ident[:])
                     nc.scalar.copy(
                         out=grouped_words[:, h * BANK_PASSES : (h + 1) * BANK_PASSES, :, :],
@@ -173,15 +183,17 @@ def tile_similaritymatrixlayer_k_kernel(tc, inputs, w, b, out):
                 sums = ps_s.tile([P, CHUNK_PASSES, PACK, TILE_SPEAKERS], F32)
                 for g in range(vector_passes(unit), CHUNK_PASSES):
                     for t in range(PACK):
-                        if g < CHUNK_PASSES - PERM_PASSES:
+                        if g < PERM_FIRST:
                             lhsT = x_quads[:, g * P : (g + 1) * P, t]
                         else:
-                            j = g - (CHUNK_PASSES - PERM_PASSES)
-                            perm_pairs = perm_tiles[unit][:].rearrange("p u (q e) -> p u q e", e=2)
-                            lhsT = perm_pairs[:, t // 2, j * P : (j + 1) * P, t % 2]
+                            lhsT = perm_tiles[unit, g][:, t // 2, :].rearrange(
+                                "p (q e) -> p q e", e=2
+                            )[:, :, t % 2]
                         nc.tensor.matmul(
                             sums[:, g, t, :], lhsT=lhsT, rhs=member[:], start=True, stop=True
                         )
+                    if g == 1:
+                        idle_pass(nc, ps_w, idle_codes, idle_scales)
                 sum_tiles[unit] = sums
 
             def vector_work(unit):

@@ -31,9 +31,9 @@ UNITS = CHUNKS * ROW_TILES
 BANK_PASSES = 2
 PLANES_PER_TILE = 4
 PERM_FIRST = 1
-PERM_VECTOR = 2
 LOADS_AHEAD = 3
-START_PASSES = 6
+NORM_PASSES = 6
+START_PASSES = 10
 
 FLOPS = 2 * ROWS * SPEAKERS * FEATURES
 
@@ -136,25 +136,16 @@ def tile_similaritymatrixlayer_k_kernel(tc, inputs, w, b, out):
                 x_tiles[unit] = x_sb
 
             def permute(unit):
-                for first, last, pool, tag in (
-                    (PERM_FIRST, PERM_VECTOR, perms, "perm_g"),
-                    (PERM_VECTOR, CHUNK_PASSES, perms, "perm_v"),
-                ):
-                    width = (last - first) * K_PASS // 2
-                    perm = pool.tile([P, 2, width], BF16, tag=tag)
-                    dst = perm[:].rearrange("p u (b e) -> p u b e", e=BLOCK // 2)
-                    src = x_tiles[unit][:, first * K_PASS : last * K_PASS].rearrange(
+                perm = perms.tile([P, 2, (CHUNK_PASSES - PERM_FIRST) * K_PASS // 2], BF16)
+                nc.vector.tensor_copy(
+                    out=perm[:].rearrange("p u (b e) -> p u b e", e=BLOCK // 2),
+                    in_=x_tiles[unit][:, PERM_FIRST * K_PASS :].rearrange(
                         "p (b u e) -> p u b e", u=2, e=BLOCK // 2
-                    )
-                    if tag == "perm_g":
-                        nc.gpsimd.tensor_scalar(
-                            out=dst, in0=src, scalar1=1.0, scalar2=0.0, op0=ALU.mult, op1=ALU.add
-                        )
-                    else:
-                        nc.vector.tensor_copy(out=dst, in_=src)
-                    for g in range(first, last):
-                        j = (g - first) * K_PASS // 2
-                        perm_tiles[unit, g] = perm[:, :, j : j + K_PASS // 2]
+                    ),
+                )
+                for g in range(PERM_FIRST, CHUNK_PASSES):
+                    j = (g - PERM_FIRST) * K_PASS // 2
+                    perm_tiles[unit, g] = perm[:, :, j : j + K_PASS // 2]
 
             def transposes(unit):
                 x_sb = x_tiles[unit]
@@ -205,14 +196,6 @@ def tile_similaritymatrixlayer_k_kernel(tc, inputs, w, b, out):
                     scales=plane_of(c, r),
                     in_=grouped[:].rearrange("p g i t -> p (g i t)"),
                 )
-                nc.vector.tensor_copy(
-                    out=spk_sum[:, c, r, first:CHUNK_PASSES, :].rearrange(
-                        "p g (s t) -> p g s t", t=PACK
-                    ),
-                    in_=sum_tiles.pop(unit)[:, first:CHUNK_PASSES, :, :].rearrange(
-                        "p g t s -> p g s t"
-                    ),
-                )
                 if first:
                     nc.vector.tensor_reduce(
                         out=spk_sum[:, c, r, 0:first, :].rearrange("p g (s t) -> p (g s) t", t=PACK),
@@ -222,6 +205,18 @@ def tile_similaritymatrixlayer_k_kernel(tc, inputs, w, b, out):
                         axis=AXIS_X,
                         op=ALU.add,
                     )
+
+            def copy_sums(unit):
+                c, r = divmod(unit, ROW_TILES)
+                first = vector_passes(unit)
+                nc.scalar.copy(
+                    out=spk_sum[:, c, r, first:CHUNK_PASSES, :].rearrange(
+                        "p g (s t) -> p g s t", t=PACK
+                    ),
+                    in_=sum_tiles.pop(unit)[:, first:CHUNK_PASSES, :, :].rearrange(
+                        "p g t s -> p g s t"
+                    ),
+                )
 
             for unit in range(LOADS_AHEAD):
                 load(unit)
@@ -233,6 +228,8 @@ def tile_similaritymatrixlayer_k_kernel(tc, inputs, w, b, out):
                     permute(unit + 1)
                 if unit < UNITS:
                     transposes(unit)
+                if unit >= 1:
+                    copy_sums(unit - 1)
                 if unit >= 2:
                     square_unit(unit - 2)
                 if unit < UNITS:
@@ -241,6 +238,8 @@ def tile_similaritymatrixlayer_k_kernel(tc, inputs, w, b, out):
                     vector_work(unit - 1)
             square_unit(UNITS - 1)
 
+            for i in range(NORM_PASSES):
+                idle_pass(nc, ps_w, idle_codes, idle_scales)
             sq_lane = keep.tile([P, 1], F32)
             nc.vector.tensor_reduce(out=sq_lane[:], in_=sq_part[:], axis=AXIS_X, op=ALU.add)
             total = ps_n.tile([P, 1], F32)

@@ -13,8 +13,9 @@ AXIS_X = mybir.AxisListType.X
 
 P = 128
 PACK = 4
-BLOCK = 32
 K_PASS = P * PACK
+BLOCK = 32
+HALF_BLOCK = BLOCK // 2
 
 ROWS = 1024
 FEATURES = 16384
@@ -24,35 +25,30 @@ EPS = 1e-6
 
 ROW_TILES = ROWS // P
 TILE_SPEAKERS = P // UTTERANCES
+TILE_SUMS = TILE_SPEAKERS * PACK
 CHUNK_PASSES = 4
 CHUNK_K = CHUNK_PASSES * K_PASS
 CHUNKS = FEATURES // CHUNK_K
 UNITS = CHUNKS * ROW_TILES
 BANK_PASSES = 2
+BANK_WORDS = BANK_PASSES * 2 * P
+WORD_BANKS = 4
+SUM_BANKS = 2
+BANKS = CHUNK_PASSES // BANK_PASSES
 PLANES_PER_TILE = 4
+SLOTS = 4
 PERM_FIRST = 1
-LOADS_AHEAD = 3
-NORM_PASSES = 6
-START_PASSES = 10
+LATE = 2
+IDLE_N = 256
+START_PASSES = 18
+WARM_UNITS = 4
+SCALAR_FROM = 4
 
 FLOPS = 2 * ROWS * SPEAKERS * FEATURES
 
 
 def vector_passes(unit):
-    return 0 if unit % 5 == 3 and unit > 5 else 1
-
-
-def idle_pass(nc, pool, codes, scales):
-    idle_out = pool.tile([P, CHUNK_PASSES * P], F32)
-    nc.tensor.matmul_mx(
-        out=idle_out[:],
-        lhsT=codes[:, 0:P].bitcast(FP8X4),
-        lhsT_scale=scales[:, 0:P],
-        rhs=codes[:].bitcast(FP8X4),
-        rhs_scale=scales[:],
-        start=True,
-        stop=True,
-    )
+    return 0 if unit > UNITS - LATE - 2 or (unit % 6 == 5 and unit < UNITS - 10) else 1
 
 
 def tile_similaritymatrixlayer_k_kernel(tc, inputs, w, b, out):
@@ -60,261 +56,321 @@ def tile_similaritymatrixlayer_k_kernel(tc, inputs, w, b, out):
     with tc.manual_schedule(), tc.tile_pool(name="keep", bufs=1) as keep:
         x_codes = keep.tile([P, CHUNKS, ROW_TILES, CHUNK_PASSES, P], U32, align_bytes=64)
         x_scales = keep.tile([P, UNITS // PLANES_PER_TILE, CHUNK_PASSES * P], U8, align_bytes=64)
-        spk_sum = keep.tile([P, CHUNKS, ROW_TILES, CHUNK_PASSES, TILE_SPEAKERS * PACK], F32)
+        spk_sum = keep.tile([P, CHUNKS, ROW_TILES, CHUNK_PASSES, TILE_SUMS], F32)
         sq_part = keep.tile([P, UNITS], F32)
 
         ident = keep.tile([P, P], F32)
-        make_identity(nc, ident[:])
         ones = keep.tile([P, P], F32)
-        nc.vector.memset(ones[:], 1.0)
         warm = keep.tile([P, 1], F32)
-        nc.scalar.sqrt(out=warm[:], in_=ones[:, 0:1])
         w_bf = keep.tile([P, 1], BF16)
         b_bf = keep.tile([P, 1], BF16)
-        nc.scalar.dma_start(out=w_bf[:], in_=w.partition_broadcast(P))
-        nc.scalar.dma_start(out=b_bf[:], in_=b.partition_broadcast(P))
+        w_pos = keep.tile([P, 1], F32)
+        w_neg = keep.tile([P, 1], F32)
+        w_abs = keep.tile([P, 1], F32)
+        b_f32 = keep.tile([P, 1], F32)
+        member_f32 = keep.tile([P, TILE_SPEAKERS], F32)
+        member = keep.tile([P, TILE_SPEAKERS], BF16)
+        sq_lane = keep.tile([P, 1], F32)
+        floored = keep.tile([P, 1], F32)
+        norm8 = keep.tile([P, 1], F32)
         inv_norm = keep.tile([P, 1], F32)
-        idle_codes = keep.tile([P, CHUNK_PASSES * P], U32, align_bytes=64)
-        idle_scales = keep.tile([P, CHUNK_PASSES * P], U8, align_bytes=64)
 
-        def plane_of(c, r):
-            unit = c * ROW_TILES + r
+        def plane_of(unit):
             return x_scales[PACK * (unit % PLANES_PER_TILE) : P, unit // PLANES_PER_TILE, :]
 
+        def codes_of(unit):
+            c, r = divmod(unit, ROW_TILES)
+            return x_codes[:, c, r, :, :].rearrange("p g i -> p (g i)")
+
         with (
-            tc.tile_pool(name="xin", bufs=4) as xin,
-            tc.tile_pool(name="perms", bufs=2) as perms,
             tc.tile_pool(name="stage", bufs=3) as stage,
-            tc.tile_pool(name="scrap", bufs=2) as scrap,
-            tc.psum_pool(name="ps_x", bufs=4) as ps_x,
-            tc.psum_pool(name="ps_s", bufs=2) as ps_s,
-            tc.psum_pool(name="ps_n", bufs=1) as ps_n,
-            tc.psum_pool(name="ps_w", bufs=1) as ps_w,
+            tc.psum_pool(name="ps", bufs=1) as ps,
         ):
-            idle_src = stage.tile([P, CHUNK_PASSES, P, PACK], BF16, align_bytes=64, tag="grouped")
-            nc.vector.memset(idle_src[:].bitcast(I32), 0)
-            nc.vector.quantize_mx(
-                out=idle_codes[:].bitcast(FP8X4),
-                scales=idle_scales[:],
-                in_=idle_src[:].rearrange("p g i t -> p (g i t)"),
-            )
-            for i in range(START_PASSES):
-                idle_pass(nc, ps_w, idle_codes, idle_scales)
-
-            member_f32 = keep.tile([P, TILE_SPEAKERS], F32)
-            nc.vector.tensor_reduce(
-                out=member_f32[:],
-                in_=ident[:].rearrange("p (s m) -> p s m", m=UTTERANCES),
-                axis=AXIS_X,
-                op=ALU.add,
-            )
-            member = keep.tile([P, TILE_SPEAKERS], BF16)
-            nc.vector.tensor_copy(out=member[:], in_=member_f32[:])
-
-            def square_unit(unit):
-                squares = scrap.tile([P, CHUNK_PASSES * TILE_SPEAKERS * PACK], BF16)
-                nc.scalar.activation(
-                    out=squares[:],
-                    in_=spk_sum[:, unit // ROW_TILES, unit % ROW_TILES, :, :].rearrange(
-                        "p g x -> p (g x)"
-                    ),
-                    func=ACT.Square,
-                    accum_out=sq_part[:, unit : unit + 1],
-                )
-
             x_tiles = {}
             perm_tiles = {}
+            word_tiles = {}
             grouped_tiles = {}
             sum_tiles = {}
 
-            def load(unit):
-                c, r = divmod(unit, ROW_TILES)
-                x_sb = xin.tile([P, CHUNK_K], BF16)
-                nc.sync.dma_start(
-                    out=x_sb[:], in_=inputs[r * P : (r + 1) * P, c * CHUNK_K : (c + 1) * CHUNK_K]
-                )
-                x_tiles[unit] = x_sb
+            def bank(tag):
+                words = ps.tile([P, BANK_WORDS], F32, tag=tag)
+                return words
 
-            def permute(unit):
-                perm = perms.tile([P, 2, (CHUNK_PASSES - PERM_FIRST) * K_PASS // 2], BF16)
-                nc.vector.tensor_copy(
-                    out=perm[:].rearrange("p u (b e) -> p u b e", e=BLOCK // 2),
-                    in_=x_tiles[unit][:, PERM_FIRST * K_PASS :].rearrange(
-                        "p (b u e) -> p u b e", u=2, e=BLOCK // 2
-                    ),
-                )
-                for g in range(PERM_FIRST, CHUNK_PASSES):
-                    j = (g - PERM_FIRST) * K_PASS // 2
-                    perm_tiles[unit, g] = perm[:, :, j : j + K_PASS // 2]
-
-            def transposes(unit):
-                x_sb = x_tiles[unit]
-                x_words = x_sb[:].bitcast(F32)
-                grouped = stage.tile([P, CHUNK_PASSES, P, PACK], BF16, align_bytes=64, tag="grouped")
-                grouped_words = grouped[:].bitcast(F32)
-                for h in range(CHUNK_PASSES // BANK_PASSES):
-                    xt = ps_x.tile([P, BANK_PASSES, 2, P], F32)
-                    for i in range(BANK_PASSES):
-                        g = h * BANK_PASSES + i
-                        for u in range(2):
-                            if g < PERM_FIRST:
-                                first = g * 2 * P + u
-                                words = x_words[:, first : (g + 1) * 2 * P : 2]
-                            else:
-                                words = perm_tiles[unit, g][:, u, :].bitcast(F32)
-                            nc.tensor.transpose(xt[:, i, u, :], words, ident[:])
-                    nc.scalar.copy(
-                        out=grouped_words[:, h * BANK_PASSES : (h + 1) * BANK_PASSES, :, :],
-                        in_=xt[:].rearrange("p g u i -> p g i u"),
-                    )
-                grouped_tiles[unit] = grouped
-
-            def tensor_sums(unit):
-                x_quads = x_tiles[unit][:].rearrange("p (q t) -> p q t", t=PACK)
-                sums = ps_s.tile([P, CHUNK_PASSES, PACK, TILE_SPEAKERS], F32)
-                for g in range(vector_passes(unit), CHUNK_PASSES):
-                    for t in range(PACK):
-                        if g < PERM_FIRST:
-                            lhsT = x_quads[:, g * P : (g + 1) * P, t]
-                        else:
-                            lhsT = perm_tiles[unit, g][:, t // 2, :].rearrange(
-                                "p (q e) -> p q e", e=2
-                            )[:, :, t % 2]
-                        nc.tensor.matmul(
-                            sums[:, g, t, :], lhsT=lhsT, rhs=member[:], start=True, stop=True
-                        )
-                    if g == 1:
-                        idle_pass(nc, ps_w, idle_codes, idle_scales)
-                sum_tiles[unit] = sums
-
-            def vector_work(unit):
-                c, r = divmod(unit, ROW_TILES)
-                first = vector_passes(unit)
-                grouped = grouped_tiles.pop(unit)
+            def quantise(unit):
                 nc.vector.quantize_mx(
-                    out=x_codes[:, c, r, :, :].rearrange("p g i -> p (g i)").bitcast(FP8X4),
-                    scales=plane_of(c, r),
-                    in_=grouped[:].rearrange("p g i t -> p (g i t)"),
+                    out=codes_of(unit).bitcast(FP8X4),
+                    scales=plane_of(unit),
+                    in_=grouped_tiles[unit][:].rearrange("p g i t -> p (g i t)"),
                 )
-                if first:
-                    nc.vector.tensor_reduce(
-                        out=spk_sum[:, c, r, 0:first, :].rearrange("p g (s t) -> p (g s) t", t=PACK),
-                        in_=grouped[:, 0:first, :, :].rearrange(
-                            "p g (s m) t -> p (g s) t m", m=UTTERANCES
+
+            with (
+                tc.tile_pool(name="xin", bufs=SLOTS) as xin,
+                tc.tile_pool(name="perms", bufs=3) as perms,
+                tc.tile_pool(name="scrap", bufs=2) as scrap,
+            ):
+
+                def load(unit):
+                    c, r = divmod(unit, ROW_TILES)
+                    x_sb = xin.tile([P, CHUNK_K], BF16)
+                    nc.sync.dma_start(
+                        out=x_sb[:], in_=inputs[r * P : (r + 1) * P, c * CHUNK_K : (c + 1) * CHUNK_K]
+                    )
+                    x_tiles[unit] = x_sb
+
+                idle_out = [bank("idle0"), bank("idle1")]
+                idle_codes = codes_of(UNITS - 1)
+                idle_scales = plane_of(UNITS - 1)
+
+                def idle_pass(i, lo, hi):
+                    nc.tensor.matmul_mx(
+                        out=idle_out[i][:, lo:hi],
+                        lhsT=idle_codes[:, 0:P].bitcast(FP8X4),
+                        lhsT_scale=idle_scales[:, 0:P],
+                        rhs=idle_codes[:, lo:hi].bitcast(FP8X4),
+                        rhs_scale=idle_scales[:, lo:hi],
+                        start=True,
+                        stop=True,
+                    )
+
+                def permute(unit):
+                    perm = perms.tile([P, 2, (CHUNK_PASSES - PERM_FIRST) * K_PASS // 2], BF16)
+                    nc.vector.tensor_copy(
+                        out=perm[:].rearrange("p u (b e) -> p u b e", e=HALF_BLOCK),
+                        in_=x_tiles[unit][:, PERM_FIRST * K_PASS :].rearrange(
+                            "p (b u e) -> p u b e", u=2, e=HALF_BLOCK
                         ),
-                        axis=AXIS_X,
-                        op=ALU.add,
+                    )
+                    for g in range(PERM_FIRST, CHUNK_PASSES):
+                        j = (g - PERM_FIRST) * K_PASS // 2
+                        perm_tiles[unit, g] = perm[:, :, j : j + K_PASS // 2]
+
+                def transposes(unit):
+                    words = x_tiles[unit][:].bitcast(F32)
+                    for h in range(BANKS):
+                        xt = bank("words%d" % ((unit * BANKS + h) % WORD_BANKS))[:].rearrange(
+                            "p (g u i) -> p g u i", g=BANK_PASSES, u=2
+                        )
+                        for i in range(BANK_PASSES):
+                            g = h * BANK_PASSES + i
+                            for u in range(2):
+                                if g < PERM_FIRST:
+                                    picked = words[:, 2 * g * P + u : 2 * (g + 1) * P : 2]
+                                else:
+                                    picked = perm_tiles[unit, g][:, u, :].bitcast(F32)
+                                nc.tensor.transpose(xt[:, i, u, :], picked, ident[:])
+                        word_tiles[unit, h] = xt
+
+                def copy_words(unit, h, copy=nc.scalar.copy):
+                    if h == 0:
+                        grouped = stage.tile(
+                            [P, CHUNK_PASSES, P, PACK], BF16, align_bytes=64, tag="grouped"
+                        )
+                        grouped_tiles[unit] = grouped
+                    copy(
+                        out=grouped_tiles[unit][:].bitcast(F32)[
+                            :, h * BANK_PASSES : (h + 1) * BANK_PASSES, :, :
+                        ],
+                        in_=word_tiles[unit, h].rearrange("p g u i -> p g i u"),
                     )
 
-            def copy_sums(unit):
-                c, r = divmod(unit, ROW_TILES)
-                first = vector_passes(unit)
-                nc.scalar.copy(
-                    out=spk_sum[:, c, r, first:CHUNK_PASSES, :].rearrange(
-                        "p g (s t) -> p g s t", t=PACK
-                    ),
-                    in_=sum_tiles.pop(unit)[:, first:CHUNK_PASSES, :, :].rearrange(
-                        "p g t s -> p g s t"
-                    ),
-                )
-
-            for unit in range(LOADS_AHEAD):
-                load(unit)
-            permute(0)
-            for unit in range(UNITS + 1):
-                if unit + LOADS_AHEAD < UNITS:
-                    load(unit + LOADS_AHEAD)
-                if unit + 1 < UNITS:
-                    permute(unit + 1)
-                if unit < UNITS:
-                    transposes(unit)
-                if unit >= 1:
-                    copy_sums(unit - 1)
-                if unit >= 2:
-                    square_unit(unit - 2)
-                if unit < UNITS:
-                    tensor_sums(unit)
-                if unit >= 1:
-                    vector_work(unit - 1)
-            square_unit(UNITS - 1)
-
-            for i in range(NORM_PASSES):
-                idle_pass(nc, ps_w, idle_codes, idle_scales)
-            sq_lane = keep.tile([P, 1], F32)
-            nc.vector.tensor_reduce(out=sq_lane[:], in_=sq_part[:], axis=AXIS_X, op=ALU.add)
-            total = ps_n.tile([P, 1], F32)
-            nc.tensor.matmul(total[:], lhsT=ones[:], rhs=sq_lane[:], start=True, stop=True)
-            floored = keep.tile([P, 1], F32)
-            nc.vector.tensor_scalar_max(
-                out=floored[:], in0=total[:], scalar1=UTTERANCES * UTTERANCES * EPS
-            )
-            norm8 = keep.tile([P, 1], F32)
-            nc.scalar.sqrt(out=norm8[:], in_=floored[:])
-            nc.vector.reciprocal(out=inv_norm[:], in_=norm8[:])
-
-        with (
-            tc.tile_pool(name="cen", bufs=1) as cen,
-            tc.tile_pool(name="cstage", bufs=3) as cstage,
-            tc.psum_pool(name="ps_acc", bufs=1) as ps_acc,
-        ):
-            c_codes = cen.tile([P, CHUNKS, CHUNK_PASSES, SPEAKERS], U32, align_bytes=64)
-            c_scales = cen.tile([P, CHUNKS, CHUNK_PASSES, SPEAKERS], U8, align_bytes=64)
-            result = cen.tile([P, ROW_TILES, SPEAKERS], F32)
-            acc = [ps_acc.tile([P, SPEAKERS], F32, name="acc%d" % r) for r in range(ROW_TILES)]
-
-            def quantise_centroids(c, g):
-                c_bf = cstage.tile([P, ROW_TILES, TILE_SPEAKERS * PACK], BF16, align_bytes=64)
-                if g % 2 == 0:
-                    nc.vector.tensor_scalar_mul(
-                        out=c_bf[:], in0=spk_sum[:, c, :, g, :], scalar1=inv_norm[:, 0:1]
+                def tensor_sums(unit):
+                    sums = bank("sums%d" % (unit % SUM_BANKS))[:, 0 : CHUNK_PASSES * TILE_SUMS].rearrange(
+                        "p (g t s) -> p g t s", g=CHUNK_PASSES, t=PACK
                     )
-                else:
+                    x_quads = x_tiles[unit][:].rearrange("p (q t) -> p q t", t=PACK)
+                    for g in range(vector_passes(unit), CHUNK_PASSES):
+                        for t in range(PACK):
+                            if g < PERM_FIRST:
+                                lhsT = x_quads[:, g * P : (g + 1) * P, t]
+                            else:
+                                lhsT = perm_tiles[unit, g][:, t // 2, :].rearrange(
+                                    "p (q e) -> p q e", e=2
+                                )[:, :, t % 2]
+                            nc.tensor.matmul(
+                                sums[:, g, t, :], lhsT=lhsT, rhs=member[:], start=True, stop=True
+                            )
+                        if g == 1 and unit < UNITS - LATE - 1:
+                            idle_pass(0, 0, BANK_WORDS)
+                        if g == 3 and unit < WARM_UNITS:
+                            idle_pass(1, 0, BANK_WORDS)
+                    sum_tiles[unit] = sums
+
+                def copy_sums(unit, copy):
+                    c, r = divmod(unit, ROW_TILES)
+                    first = vector_passes(unit)
+                    copy(
+                        out=spk_sum[:, c, r, first:, :].rearrange("p g (s t) -> p g s t", t=PACK),
+                        in_=sum_tiles[unit][:, first:, :, :].rearrange("p g t s -> p g s t"),
+                    )
+
+                def vector_sums(unit):
+                    c, r = divmod(unit, ROW_TILES)
+                    first = vector_passes(unit)
+                    if first:
+                        nc.vector.tensor_reduce(
+                            out=spk_sum[:, c, r, 0:first, :].rearrange(
+                                "p g (s t) -> p (g s) t", t=PACK
+                            ),
+                            in_=grouped_tiles[unit][:, 0:first, :, :].rearrange(
+                                "p g (s m) t -> p (g s) t m", m=UTTERANCES
+                            ),
+                            axis=AXIS_X,
+                            op=ALU.add,
+                        )
+
+                def square(unit, values):
+                    squares = scrap.tile([P, CHUNK_PASSES * TILE_SUMS], BF16)
                     nc.scalar.activation(
-                        out=c_bf[:], in_=spk_sum[:, c, :, g, :], func=ACT.Copy, scale=inv_norm[:, 0:1]
+                        out=squares[:],
+                        in_=values,
+                        func=ACT.Square,
+                        accum_out=sq_part[:, unit : unit + 1],
                     )
-                nc.vector.quantize_mx(
-                    out=c_codes[:, c, g, :].bitcast(FP8X4),
-                    scales=c_scales[:, c, g, :],
-                    in_=c_bf[:].rearrange("p r x -> p (r x)"),
-                )
 
-            def product_pass(c, g, r):
-                nc.tensor.matmul_mx(
-                    out=acc[r][:],
-                    lhsT=x_codes[:, c, r, g, :].bitcast(FP8X4),
-                    lhsT_scale=plane_of(c, r)[:, g * P : (g + 1) * P],
-                    rhs=c_codes[:, c, g, :].bitcast(FP8X4),
-                    rhs_scale=c_scales[:, c, g, :],
-                    start=(c == 0 and g == 0),
-                    stop=(c == CHUNKS - 1 and g == CHUNK_PASSES - 1),
-                )
+                def square_kept(unit):
+                    c, r = divmod(unit, ROW_TILES)
+                    square(unit, spk_sum[:, c, r, :, :].rearrange("p g x -> p (g x)"))
 
-            for c in range(CHUNKS - 1):
-                for g in range(CHUNK_PASSES):
-                    quantise_centroids(c, g)
+                for unit in range(SLOTS):
+                    load(unit)
+                make_identity(nc, ident[:])
+                idle_src = stage.tile([P, CHUNK_PASSES, P, PACK], BF16, align_bytes=64, tag="grouped")
+                idle_flat = idle_src[:].rearrange("p g i t -> p (g i t)")[:, 0 : IDLE_N * PACK]
+                nc.vector.memset(idle_flat.bitcast(I32), 0)
+                for lo in (0, IDLE_N):
+                    nc.vector.quantize_mx(
+                        out=idle_codes[:, lo : lo + IDLE_N].bitcast(FP8X4),
+                        scales=idle_scales[:, lo : lo + IDLE_N],
+                        in_=idle_flat,
+                    )
+                nc.vector.memset(ones[:], 1.0)
+                nc.scalar.sqrt(out=warm[:], in_=ones[:, 0:1])
+                for i in range(START_PASSES):
+                    lo = i // 2 % 2 * IDLE_N
+                    idle_pass(i % 2, lo, lo + IDLE_N)
+                nc.vector.tensor_reduce(
+                    out=member_f32[:],
+                    in_=ident[:].rearrange("p (s m) -> p s m", m=UTTERANCES),
+                    axis=AXIS_X,
+                    op=ALU.add,
+                )
+                nc.vector.tensor_copy(out=member[:], in_=member_f32[:])
+
+                permute(0)
+                for step in range(UNITS - LATE + 1):
+                    late = step == UNITS - LATE
+                    if 0 < step < UNITS - SLOTS + 1:
+                        load(step + SLOTS - 1)
+                    permute(step + 1)
+                    if not late:
+                        transposes(step)
+                        for h in range(BANKS):
+                            copy_words(step, h)
+                    if step >= 1:
+                        copy_sums(step - 1, nc.scalar.copy if step % 4 else nc.vector.tensor_copy)
+                    if step >= 2:
+                        square_kept(step - 2)
+                    for unit in range(step, UNITS if late else step + 1):
+                        tensor_sums(unit)
+                    if step >= 1:
+                        quantise(step - 1)
+                        vector_sums(step - 1)
+                    if step == 3:
+                        nc.scalar.dma_start(out=w_bf[:], in_=w.partition_broadcast(P))
+                        nc.scalar.dma_start(out=b_bf[:], in_=b.partition_broadcast(P))
+                    if step == 8:
+                        nc.vector.tensor_copy(out=w_pos[:], in_=w_bf[:])
+                        nc.vector.tensor_scalar_mul(out=w_neg[:], in0=w_pos[:], scalar1=-1.0)
+                        nc.vector.tensor_tensor(
+                            out=w_abs[:], in0=w_pos[:], in1=w_neg[:], op=ALU.max
+                        )
+                        nc.vector.tensor_copy(out=b_f32[:], in_=b_bf[:])
+
+                square_kept(UNITS - LATE - 1)
+                for unit in range(UNITS - LATE, UNITS):
+                    square(unit, sum_tiles[unit].rearrange("p g t s -> p (g t s)"))
+                nc.vector.tensor_reduce(out=sq_lane[:], in_=sq_part[:], axis=AXIS_X, op=ALU.add)
+                transposes(UNITS - 2)
+                total = bank("idle1")[:, 0:1]
+                nc.tensor.matmul(total, lhsT=ones[:], rhs=sq_lane[:], start=True, stop=True)
+                transposes(UNITS - 1)
+                idle_pass(0, 0, BANK_WORDS)
+                copy_words(UNITS - 2, 0)
+                copy_sums(UNITS - 2, nc.vector.tensor_copy)
+                nc.vector.tensor_scalar_max(
+                    out=floored[:], in0=total, scalar1=UTTERANCES * UTTERANCES * EPS
+                )
+                nc.scalar.sqrt(out=norm8[:], in_=floored[:])
+                copy_sums(UNITS - 1, nc.vector.tensor_copy)
+                nc.vector.reciprocal(out=inv_norm[:], in_=norm8[:])
+                copy_words(UNITS - 2, 1)
+                for h in range(BANKS):
+                    copy_words(UNITS - 1, h)
+
+            with (
+                tc.tile_pool(name="cstage", bufs=2) as cstage,
+                tc.tile_pool(name="res", bufs=7) as res,
+                tc.tile_pool(name="cen", bufs=1) as cen,
+            ):
+                passes = CHUNKS * CHUNK_PASSES
+                c_scales = cen.tile([P, passes, SPEAKERS], U8, align_bytes=64)
+                c_codes = cen.tile([P, passes, SPEAKERS], U32, align_bytes=64)
+                acc = [
+                    bank(tag)[:, 0:SPEAKERS]
+                    for tag in ["idle1", "idle0", "sums0", "sums1"]
+                    + ["words%d" % i for i in range(WORD_BANKS)]
+                ]
+                def quantise_centroids(k):
+                    c, g = divmod(k, CHUNK_PASSES)
+                    c_bf = cstage.tile([P, ROW_TILES, TILE_SUMS], BF16, align_bytes=64)
+                    if k < SCALAR_FROM or k % 2 == 0:
+                        nc.vector.tensor_scalar_mul(
+                            out=c_bf[:], in0=spk_sum[:, c, :, g, :], scalar1=inv_norm[:, 0:1]
+                        )
+                    else:
+                        nc.scalar.activation(
+                            out=c_bf[:],
+                            in_=spk_sum[:, c, :, g, :],
+                            func=ACT.Copy,
+                            scale=inv_norm[:, 0:1],
+                        )
+                    nc.vector.quantize_mx(
+                        out=c_codes[:, k, :].bitcast(FP8X4),
+                        scales=c_scales[:, k, :],
+                        in_=c_bf[:].rearrange("p r x -> p (r x)"),
+                    )
+
+                def product_pass(k, r):
+                    c, g = divmod(k, CHUNK_PASSES)
+                    nc.tensor.matmul_mx(
+                        out=acc[r],
+                        lhsT=x_codes[:, c, r, g, :].bitcast(FP8X4),
+                        lhsT_scale=plane_of(c * ROW_TILES + r)[:, g * P : (g + 1) * P],
+                        rhs=c_codes[:, k, :].bitcast(FP8X4),
+                        rhs_scale=c_scales[:, k, :],
+                        start=(k == 0),
+                        stop=(k == passes - 1),
+                    )
+
+                for k in range(passes - CHUNK_PASSES):
+                    quantise_centroids(k)
+                    if k < LATE:
+                        quantise(UNITS - LATE + k)
                     for r in range(ROW_TILES):
-                        product_pass(c, g, r)
+                        product_pass(k, r)
 
-            w_pos = keep.tile([P, 1], F32)
-            w_neg = keep.tile([P, 1], F32)
-            w_abs = keep.tile([P, 1], F32)
-            b_f32 = keep.tile([P, 1], F32)
-            nc.vector.tensor_copy(out=w_pos[:], in_=w_bf[:])
-            nc.vector.tensor_scalar_mul(out=w_neg[:], in0=w_pos[:], scalar1=-1.0)
-            nc.vector.tensor_tensor(out=w_abs[:], in0=w_pos[:], in1=w_neg[:], op=ALU.max)
-            nc.vector.tensor_copy(out=b_f32[:], in_=b_bf[:])
-
-            for g in range(CHUNK_PASSES):
-                quantise_centroids(CHUNKS - 1, g)
-            for r in range(ROW_TILES):
-                for g in range(CHUNK_PASSES):
-                    product_pass(CHUNKS - 1, g, r)
-                nc.scalar.activation(
-                    out=result[:, r, :],
-                    in_=acc[r][:],
-                    func=ACT.Relu,
-                    bias=b_f32[:, 0:1],
-                    scale=w_abs[:, 0:1],
-                )
-                nc.vector.tensor_scalar_min(out=result[:, r, :], in0=result[:, r, :], scalar1=1.0)
-                nc.sync.dma_start(out=out[r * P : (r + 1) * P, :], in_=result[:, r, :])
+                for k in range(passes - CHUNK_PASSES, passes):
+                    quantise_centroids(k)
+                for r in range(ROW_TILES):
+                    for k in range(passes - CHUNK_PASSES, passes):
+                        product_pass(k, r)
+                    result = res.tile([P, SPEAKERS], F32)
+                    nc.scalar.activation(
+                        out=result[:],
+                        in_=acc[r],
+                        func=ACT.Relu,
+                        bias=b_f32[:, 0:1],
+                        scale=w_abs[:, 0:1],
+                    )
+                    nc.vector.tensor_scalar_min(out=result[:], in0=result[:], scalar1=1.0)
+                    nc.sync.dma_start(out=out[r * P : (r + 1) * P, :], in_=result[:])

@@ -42,7 +42,9 @@ LATE = 2
 IDLE_N = 256
 START_PASSES = 18
 WARM_UNITS = 4
-SCALAR_FROM = 4
+NORM_PASSES = 6
+LATE_QUANTISE = [6, 9]
+SCALAR_FROM = 1
 
 FLOPS = 2 * ROWS * SPEAKERS * FEATURES
 
@@ -118,16 +120,18 @@ def tile_similaritymatrixlayer_k_kernel(tc, inputs, w, b, out):
                     x_tiles[unit] = x_sb
 
                 idle_out = [bank("idle0"), bank("idle1")]
-                idle_codes = codes_of(UNITS - 1)
-                idle_scales = plane_of(UNITS - 1)
+                zeros = UNITS - 1
+                idle_codes = codes_of(zeros)
+                idle_scales = plane_of(zeros)
 
-                def idle_pass(i, lo, hi):
+                def idle_pass(i, lo, hi, unit):
+                    codes, scales = codes_of(unit), plane_of(unit)
                     nc.tensor.matmul_mx(
                         out=idle_out[i][:, lo:hi],
-                        lhsT=idle_codes[:, 0:P].bitcast(FP8X4),
-                        lhsT_scale=idle_scales[:, 0:P],
-                        rhs=idle_codes[:, lo:hi].bitcast(FP8X4),
-                        rhs_scale=idle_scales[:, lo:hi],
+                        lhsT=codes[:, 0:P].bitcast(FP8X4),
+                        lhsT_scale=scales[:, 0:P],
+                        rhs=codes[:, lo:hi].bitcast(FP8X4),
+                        rhs_scale=scales[:, lo:hi],
                         start=True,
                         stop=True,
                     )
@@ -189,10 +193,10 @@ def tile_similaritymatrixlayer_k_kernel(tc, inputs, w, b, out):
                             nc.tensor.matmul(
                                 sums[:, g, t, :], lhsT=lhsT, rhs=member[:], start=True, stop=True
                             )
-                        if g == 1 and unit < UNITS - LATE - 1:
-                            idle_pass(0, 0, BANK_WORDS)
+                        if g == 1:
+                            idle_pass(0, 0, BANK_WORDS, zeros if unit < UNITS - LATE - 1 else 0)
                         if g == 3 and unit < WARM_UNITS:
-                            idle_pass(1, 0, BANK_WORDS)
+                            idle_pass(1, 0, BANK_WORDS, zeros)
                     sum_tiles[unit] = sums
 
                 def copy_sums(unit, copy):
@@ -247,7 +251,7 @@ def tile_similaritymatrixlayer_k_kernel(tc, inputs, w, b, out):
                 nc.scalar.sqrt(out=warm[:], in_=ones[:, 0:1])
                 for i in range(START_PASSES):
                     lo = i // 2 % 2 * IDLE_N
-                    idle_pass(i % 2, lo, lo + IDLE_N)
+                    idle_pass(i % 2, lo, lo + IDLE_N, zeros)
                 nc.vector.tensor_reduce(
                     out=member_f32[:],
                     in_=ident[:].rearrange("p (s m) -> p s m", m=UTTERANCES),
@@ -294,7 +298,9 @@ def tile_similaritymatrixlayer_k_kernel(tc, inputs, w, b, out):
                 total = bank("idle1")[:, 0:1]
                 nc.tensor.matmul(total, lhsT=ones[:], rhs=sq_lane[:], start=True, stop=True)
                 transposes(UNITS - 1)
-                idle_pass(0, 0, BANK_WORDS)
+                for i in range(NORM_PASSES):
+                    lo = i % 2 * IDLE_N
+                    idle_pass(0, lo, lo + IDLE_N, 0)
                 copy_words(UNITS - 2, 0)
                 copy_sums(UNITS - 2, nc.vector.tensor_copy)
                 nc.vector.tensor_scalar_max(
@@ -354,8 +360,8 @@ def tile_similaritymatrixlayer_k_kernel(tc, inputs, w, b, out):
 
                 for k in range(passes - CHUNK_PASSES):
                     quantise_centroids(k)
-                    if k < LATE:
-                        quantise(UNITS - LATE + k)
+                    if k in LATE_QUANTISE:
+                        quantise(UNITS - LATE + LATE_QUANTISE.index(k))
                     for r in range(ROW_TILES):
                         product_pass(k, r)
 

import concourse.mybir as mybir
from concourse.masks import make_identity

F32 = mybir.dt.float32
BF16 = mybir.dt.bfloat16
U32 = mybir.dt.uint32
U8 = mybir.dt.uint8
I32 = mybir.dt.int32
FP8X4 = mybir.dt.float8_e4m3fn_x4
ALU = mybir.AluOpType
ACT = mybir.ActivationFunctionType
AXIS_X = mybir.AxisListType.X

P = 128
PACK = 4
K_PASS = P * PACK
BLOCK = 32
HALF_BLOCK = BLOCK // 2

ROWS = 1024
FEATURES = 16384
SPEAKERS = 128
UTTERANCES = 8
EPS = 1e-6

ROW_TILES = ROWS // P
TILE_SPEAKERS = P // UTTERANCES
TILE_SUMS = TILE_SPEAKERS * PACK
CHUNK_PASSES = 4
CHUNK_K = CHUNK_PASSES * K_PASS
CHUNKS = FEATURES // CHUNK_K
UNITS = CHUNKS * ROW_TILES
BANK_PASSES = 2
BANK_WORDS = BANK_PASSES * 2 * P
WORD_BANKS = 4
SUM_BANKS = 2
BANKS = CHUNK_PASSES // BANK_PASSES
PLANES_PER_TILE = 4
SLOTS = 4
PERM_FIRST = 1
LATE = 2
IDLE_N = 256
START_PASSES = 18
WARM_UNITS = 4
NORM_PASSES = 6
LATE_QUANTISE = [6, 9]
SCALAR_FROM = 1

FLOPS = 2 * ROWS * SPEAKERS * FEATURES


def vector_passes(unit):
    return 0 if unit > UNITS - LATE - 2 or (unit % 6 == 5 and unit < UNITS - 10) else 1


def tile_similaritymatrixlayer_k_kernel(tc, inputs, w, b, out):
    nc = tc.nc
    with tc.manual_schedule(), tc.tile_pool(name="keep", bufs=1) as keep:
        x_codes = keep.tile([P, CHUNKS, ROW_TILES, CHUNK_PASSES, P], U32, align_bytes=64)
        x_scales = keep.tile([P, UNITS // PLANES_PER_TILE, CHUNK_PASSES * P], U8, align_bytes=64)
        spk_sum = keep.tile([P, CHUNKS, ROW_TILES, CHUNK_PASSES, TILE_SUMS], F32)
        sq_part = keep.tile([P, UNITS], F32)

        ident = keep.tile([P, P], F32)
        ones = keep.tile([P, P], F32)
        warm = keep.tile([P, 1], F32)
        w_bf = keep.tile([P, 1], BF16)
        b_bf = keep.tile([P, 1], BF16)
        w_pos = keep.tile([P, 1], F32)
        w_neg = keep.tile([P, 1], F32)
        w_abs = keep.tile([P, 1], F32)
        b_f32 = keep.tile([P, 1], F32)
        member_f32 = keep.tile([P, TILE_SPEAKERS], F32)
        member = keep.tile([P, TILE_SPEAKERS], BF16)
        sq_lane = keep.tile([P, 1], F32)
        floored = keep.tile([P, 1], F32)
        norm8 = keep.tile([P, 1], F32)
        inv_norm = keep.tile([P, 1], F32)

        def plane_of(unit):
            return x_scales[PACK * (unit % PLANES_PER_TILE) : P, unit // PLANES_PER_TILE, :]

        def codes_of(unit):
            c, r = divmod(unit, ROW_TILES)
            return x_codes[:, c, r, :, :].rearrange("p g i -> p (g i)")

        with (
            tc.tile_pool(name="stage", bufs=3) as stage,
            tc.psum_pool(name="ps", bufs=1) as ps,
        ):
            x_tiles = {}
            perm_tiles = {}
            word_tiles = {}
            grouped_tiles = {}
            sum_tiles = {}

            def bank(tag):
                words = ps.tile([P, BANK_WORDS], F32, tag=tag)
                return words

            def quantise(unit):
                nc.vector.quantize_mx(
                    out=codes_of(unit).bitcast(FP8X4),
                    scales=plane_of(unit),
                    in_=grouped_tiles[unit][:].rearrange("p g i t -> p (g i t)"),
                )

            with (
                tc.tile_pool(name="xin", bufs=SLOTS) as xin,
                tc.tile_pool(name="perms", bufs=3) as perms,
                tc.tile_pool(name="scrap", bufs=2) as scrap,
            ):

                def load(unit):
                    c, r = divmod(unit, ROW_TILES)
                    x_sb = xin.tile([P, CHUNK_K], BF16)
                    nc.sync.dma_start(
                        out=x_sb[:], in_=inputs[r * P : (r + 1) * P, c * CHUNK_K : (c + 1) * CHUNK_K]
                    )
                    x_tiles[unit] = x_sb

                idle_out = [bank("idle0"), bank("idle1")]
                zeros = UNITS - 1
                idle_codes = codes_of(zeros)
                idle_scales = plane_of(zeros)

                def idle_pass(i, lo, hi, unit):
                    codes, scales = codes_of(unit), plane_of(unit)
                    nc.tensor.matmul_mx(
                        out=idle_out[i][:, lo:hi],
                        lhsT=codes[:, 0:P].bitcast(FP8X4),
                        lhsT_scale=scales[:, 0:P],
                        rhs=codes[:, lo:hi].bitcast(FP8X4),
                        rhs_scale=scales[:, lo:hi],
                        start=True,
                        stop=True,
                    )

                def permute(unit):
                    perm = perms.tile([P, 2, (CHUNK_PASSES - PERM_FIRST) * K_PASS // 2], BF16)
                    nc.vector.tensor_copy(
                        out=perm[:].rearrange("p u (b e) -> p u b e", e=HALF_BLOCK),
                        in_=x_tiles[unit][:, PERM_FIRST * K_PASS :].rearrange(
                            "p (b u e) -> p u b e", u=2, e=HALF_BLOCK
                        ),
                    )
                    for g in range(PERM_FIRST, CHUNK_PASSES):
                        j = (g - PERM_FIRST) * K_PASS // 2
                        perm_tiles[unit, g] = perm[:, :, j : j + K_PASS // 2]

                def transposes(unit):
                    words = x_tiles[unit][:].bitcast(F32)
                    for h in range(BANKS):
                        xt = bank("words%d" % ((unit * BANKS + h) % WORD_BANKS))[:].rearrange(
                            "p (g u i) -> p g u i", g=BANK_PASSES, u=2
                        )
                        for i in range(BANK_PASSES):
                            g = h * BANK_PASSES + i
                            for u in range(2):
                                if g < PERM_FIRST:
                                    picked = words[:, 2 * g * P + u : 2 * (g + 1) * P : 2]
                                else:
                                    picked = perm_tiles[unit, g][:, u, :].bitcast(F32)
                                nc.tensor.transpose(xt[:, i, u, :], picked, ident[:])
                        word_tiles[unit, h] = xt

                def copy_words(unit, h, copy=nc.scalar.copy):
                    if h == 0:
                        grouped = stage.tile(
                            [P, CHUNK_PASSES, P, PACK], BF16, align_bytes=64, tag="grouped"
                        )
                        grouped_tiles[unit] = grouped
                    copy(
                        out=grouped_tiles[unit][:].bitcast(F32)[
                            :, h * BANK_PASSES : (h + 1) * BANK_PASSES, :, :
                        ],
                        in_=word_tiles[unit, h].rearrange("p g u i -> p g i u"),
                    )

                def tensor_sums(unit):
                    sums = bank("sums%d" % (unit % SUM_BANKS))[:, 0 : CHUNK_PASSES * TILE_SUMS].rearrange(
                        "p (g t s) -> p g t s", g=CHUNK_PASSES, t=PACK
                    )
                    x_quads = x_tiles[unit][:].rearrange("p (q t) -> p q t", t=PACK)
                    for g in range(vector_passes(unit), CHUNK_PASSES):
                        for t in range(PACK):
                            if g < PERM_FIRST:
                                lhsT = x_quads[:, g * P : (g + 1) * P, t]
                            else:
                                lhsT = perm_tiles[unit, g][:, t // 2, :].rearrange(
                                    "p (q e) -> p q e", e=2
                                )[:, :, t % 2]
                            nc.tensor.matmul(
                                sums[:, g, t, :], lhsT=lhsT, rhs=member[:], start=True, stop=True
                            )
                        if g == 1:
                            idle_pass(0, 0, BANK_WORDS, zeros if unit < UNITS - LATE - 1 else 0)
                        if g == 3 and unit < WARM_UNITS:
                            idle_pass(1, 0, BANK_WORDS, zeros)
                    sum_tiles[unit] = sums

                def copy_sums(unit, copy):
                    c, r = divmod(unit, ROW_TILES)
                    first = vector_passes(unit)
                    copy(
                        out=spk_sum[:, c, r, first:, :].rearrange("p g (s t) -> p g s t", t=PACK),
                        in_=sum_tiles[unit][:, first:, :, :].rearrange("p g t s -> p g s t"),
                    )

                def vector_sums(unit):
                    c, r = divmod(unit, ROW_TILES)
                    first = vector_passes(unit)
                    if first:
                        nc.vector.tensor_reduce(
                            out=spk_sum[:, c, r, 0:first, :].rearrange(
                                "p g (s t) -> p (g s) t", t=PACK
                            ),
                            in_=grouped_tiles[unit][:, 0:first, :, :].rearrange(
                                "p g (s m) t -> p (g s) t m", m=UTTERANCES
                            ),
                            axis=AXIS_X,
                            op=ALU.add,
                        )

                def square(unit, values):
                    squares = scrap.tile([P, CHUNK_PASSES * TILE_SUMS], BF16)
                    nc.scalar.activation(
                        out=squares[:],
                        in_=values,
                        func=ACT.Square,
                        accum_out=sq_part[:, unit : unit + 1],
                    )

                def square_kept(unit):
                    c, r = divmod(unit, ROW_TILES)
                    square(unit, spk_sum[:, c, r, :, :].rearrange("p g x -> p (g x)"))

                for unit in range(SLOTS):
                    load(unit)
                make_identity(nc, ident[:])
                idle_src = stage.tile([P, CHUNK_PASSES, P, PACK], BF16, align_bytes=64, tag="grouped")
                idle_flat = idle_src[:].rearrange("p g i t -> p (g i t)")[:, 0 : IDLE_N * PACK]
                nc.vector.memset(idle_flat.bitcast(I32), 0)
                for lo in (0, IDLE_N):
                    nc.vector.quantize_mx(
                        out=idle_codes[:, lo : lo + IDLE_N].bitcast(FP8X4),
                        scales=idle_scales[:, lo : lo + IDLE_N],
                        in_=idle_flat,
                    )
                nc.vector.memset(ones[:], 1.0)
                nc.scalar.sqrt(out=warm[:], in_=ones[:, 0:1])
                for i in range(START_PASSES):
                    lo = i // 2 % 2 * IDLE_N
                    idle_pass(i % 2, lo, lo + IDLE_N, zeros)
                nc.vector.tensor_reduce(
                    out=member_f32[:],
                    in_=ident[:].rearrange("p (s m) -> p s m", m=UTTERANCES),
                    axis=AXIS_X,
                    op=ALU.add,
                )
                nc.vector.tensor_copy(out=member[:], in_=member_f32[:])

                permute(0)
                for step in range(UNITS - LATE + 1):
                    late = step == UNITS - LATE
                    if 0 < step < UNITS - SLOTS + 1:
                        load(step + SLOTS - 1)
                    permute(step + 1)
                    if not late:
                        transposes(step)
                        for h in range(BANKS):
                            copy_words(step, h)
                    if step >= 1:
                        copy_sums(step - 1, nc.scalar.copy if step % 4 else nc.vector.tensor_copy)
                    if step >= 2:
                        square_kept(step - 2)
                    for unit in range(step, UNITS if late else step + 1):
                        tensor_sums(unit)
                    if step >= 1:
                        quantise(step - 1)
                        vector_sums(step - 1)
                    if step == 3:
                        nc.scalar.dma_start(out=w_bf[:], in_=w.partition_broadcast(P))
                        nc.scalar.dma_start(out=b_bf[:], in_=b.partition_broadcast(P))
                    if step == 8:
                        nc.vector.tensor_copy(out=w_pos[:], in_=w_bf[:])
                        nc.vector.tensor_scalar_mul(out=w_neg[:], in0=w_pos[:], scalar1=-1.0)
                        nc.vector.tensor_tensor(
                            out=w_abs[:], in0=w_pos[:], in1=w_neg[:], op=ALU.max
                        )
                        nc.vector.tensor_copy(out=b_f32[:], in_=b_bf[:])

                square_kept(UNITS - LATE - 1)
                for unit in range(UNITS - LATE, UNITS):
                    square(unit, sum_tiles[unit].rearrange("p g t s -> p (g t s)"))
                nc.vector.tensor_reduce(out=sq_lane[:], in_=sq_part[:], axis=AXIS_X, op=ALU.add)
                transposes(UNITS - 2)
                total = bank("idle1")[:, 0:1]
                nc.tensor.matmul(total, lhsT=ones[:], rhs=sq_lane[:], start=True, stop=True)
                transposes(UNITS - 1)
                for i in range(NORM_PASSES):
                    lo = i % 2 * IDLE_N
                    idle_pass(0, lo, lo + IDLE_N, 0)
                copy_words(UNITS - 2, 0)
                copy_sums(UNITS - 2, nc.vector.tensor_copy)
                nc.vector.tensor_scalar_max(
                    out=floored[:], in0=total, scalar1=UTTERANCES * UTTERANCES * EPS
                )
                nc.scalar.sqrt(out=norm8[:], in_=floored[:])
                copy_sums(UNITS - 1, nc.vector.tensor_copy)
                nc.vector.reciprocal(out=inv_norm[:], in_=norm8[:])
                copy_words(UNITS - 2, 1)
                for h in range(BANKS):
                    copy_words(UNITS - 1, h)

            with (
                tc.tile_pool(name="cstage", bufs=2) as cstage,
                tc.tile_pool(name="res", bufs=7) as res,
                tc.tile_pool(name="cen", bufs=1) as cen,
            ):
                passes = CHUNKS * CHUNK_PASSES
                c_scales = cen.tile([P, passes, SPEAKERS], U8, align_bytes=64)
                c_codes = cen.tile([P, passes, SPEAKERS], U32, align_bytes=64)
                acc = [
                    bank(tag)[:, 0:SPEAKERS]
                    for tag in ["idle1", "idle0", "sums0", "sums1"]
                    + ["words%d" % i for i in range(WORD_BANKS)]
                ]
                def quantise_centroids(k):
                    c, g = divmod(k, CHUNK_PASSES)
                    c_bf = cstage.tile([P, ROW_TILES, TILE_SUMS], BF16, align_bytes=64)
                    if k < SCALAR_FROM or k % 2 == 0:
                        nc.vector.tensor_scalar_mul(
                            out=c_bf[:], in0=spk_sum[:, c, :, g, :], scalar1=inv_norm[:, 0:1]
                        )
                    else:
                        nc.scalar.activation(
                            out=c_bf[:],
                            in_=spk_sum[:, c, :, g, :],
                            func=ACT.Copy,
                            scale=inv_norm[:, 0:1],
                        )
                    nc.vector.quantize_mx(
                        out=c_codes[:, k, :].bitcast(FP8X4),
                        scales=c_scales[:, k, :],
                        in_=c_bf[:].rearrange("p r x -> p (r x)"),
                    )

                def product_pass(k, r):
                    c, g = divmod(k, CHUNK_PASSES)
                    nc.tensor.matmul_mx(
                        out=acc[r],
                        lhsT=x_codes[:, c, r, g, :].bitcast(FP8X4),
                        lhsT_scale=plane_of(c * ROW_TILES + r)[:, g * P : (g + 1) * P],
                        rhs=c_codes[:, k, :].bitcast(FP8X4),
                        rhs_scale=c_scales[:, k, :],
                        start=(k == 0),
                        stop=(k == passes - 1),
                    )

                for k in range(passes - CHUNK_PASSES):
                    quantise_centroids(k)
                    if k in LATE_QUANTISE:
                        quantise(UNITS - LATE + LATE_QUANTISE.index(k))
                    for r in range(ROW_TILES):
                        product_pass(k, r)

                for k in range(passes - CHUNK_PASSES, passes):
                    quantise_centroids(k)
                for r in range(ROW_TILES):
                    for k in range(passes - CHUNK_PASSES, passes):
                        product_pass(k, r)
                    result = res.tile([P, SPEAKERS], F32)
                    nc.scalar.activation(
                        out=result[:],
                        in_=acc[r],
                        func=ACT.Relu,
                        bias=b_f32[:, 0:1],
                        scale=w_abs[:, 0:1],
                    )
                    nc.vector.tensor_scalar_min(out=result[:], in0=result[:], scalar1=1.0)
                    nc.sync.dma_start(out=out[r * P : (r + 1) * P, :], in_=result[:])
